import numpy as np
import ml_dtypes


def mxq(x, axis, fmt="e4m3"):
    dtype, down = {"e4m3": (ml_dtypes.float8_e4m3fn, 7), "e5m2": (ml_dtypes.float8_e5m2, 14)}[fmt]
    v = np.moveaxis(np.asarray(x, np.float32).astype(ml_dtypes.bfloat16).astype(np.float64), axis, -1)
    blocks = v.reshape(v.shape[:-1] + (-1, 32))
    amax = np.abs(blocks).max(-1, keepdims=True)
    byte = np.maximum(np.where(amax > 0, np.frexp(amax)[1] - 1 + 127, 0) - down, 1)
    scale = np.exp2(byte - 127.0)
    codes = (blocks / scale).astype(np.float32).astype(dtype).astype(np.float64)
    return np.moveaxis((codes * scale).reshape(v.shape), -1, axis)


WIDE = False


def mx_kscale(k):
    if not WIDE:
        return np.ones(k)
    levels = np.array([10, -10, 5, -5, 0])
    if k % 512:
        return np.exp2(np.random.permutation(np.resize(levels, k // 32))).repeat(32)
    a = np.empty((k // 512, 16))
    for p in range(k // 512):
        a[p, :8] = np.random.permutation(np.resize(levels, 8))
        for g in range(8):
            far = levels[np.abs(levels - a[p, g]) >= 10]
            a[p, g + 8] = far[np.random.randint(len(far))]
    return np.exp2(a.ravel()).repeat(32)


BF16 = ml_dtypes.bfloat16


def bf(x):
    return np.asarray(x, np.float32).astype(BF16)


def f64(x):
    return np.asarray(x).astype(np.float64)


B, STACK, TUBE, CH, IMG, PATCH, EMBED = 4, 16, 2, 1, 256, 64, 512
GH = IMG // PATCH
GW = IMG // PATCH
GD = STACK // TUBE
K = TUBE * CH * PATCH * PATCH


def _sincos_1d(dim, pos):
    omega = 1.0 / (10000.0 ** (np.arange(dim // 2, dtype=np.float64) / (dim / 2.0)))
    out = pos[:, None].astype(np.float64) * omega[None, :]
    return np.concatenate([np.sin(out), np.cos(out)], axis=1)


def get_3d_sincos_pos_embed(grid_h, grid_w, grid_depth, embed_dim):
    dim_t = embed_dim // 4
    dim_s = embed_dim - dim_t
    emb_t = _sincos_1d(dim_t, np.arange(grid_depth))
    emb_h = _sincos_1d(dim_s // 2, np.arange(grid_h))
    emb_w = _sincos_1d(dim_s - dim_s // 2, np.arange(grid_w))
    emb_hw = np.concatenate([np.repeat(emb_h, grid_w, axis=0), np.tile(emb_w, (grid_h, 1))], axis=1)
    ns = grid_h * grid_w
    return np.concatenate([np.repeat(emb_t, ns, axis=0), np.tile(emb_hw, (grid_depth, 1))], axis=1)


def setup_inputs():
    s = mx_kscale(K)
    sv = s.reshape(TUBE, CH, PATCH, PATCH)[:, :, None, :, None, :]
    video = np.random.standard_normal((B, GD, TUBE, CH, GH, PATCH, GW, PATCH)) * sv
    return {"video": bf(video.reshape(B, STACK, CH, IMG, IMG)),
            "W": bf(np.random.standard_normal((EMBED, K)) / np.sqrt(K) / s[None, :]),
            "b": bf(np.random.standard_normal(EMBED) * 0.3),
            "pos_embed": bf(get_3d_sincos_pos_embed(GH, GW, GD, EMBED)[None])}


def reference(video, W, b, pos_embed):
    video = f64(video)
    B_, T, C, H, W_ = video.shape
    p = PATCH
    gh, gw = H // p, W_ // p
    ns = gh * gw
    x = video.reshape(B_ * T, C, gh, p, gw, p)
    x = x.transpose(0, 2, 4, 1, 3, 5)
    x = x.reshape(B_, T, ns, C * p * p)
    x = x.reshape(B_, GD, TUBE, ns, C * p * p)
    x = x.transpose(0, 1, 3, 2, 4)
    tubelets = x.reshape(B_, GD * ns, TUBE * C * p * p)
    tokens = (mxq(tubelets, 2, "e4m3") @ mxq(f64(W), 1, "e4m3").T) + f64(b) + f64(pos_embed)
    return tokens

@@ -1,0 +1,171 @@
+from contextlib import ExitStack
+
+import concourse.mybir as mybir
+from concourse.masks import make_identity
+
+BF16 = mybir.dt.bfloat16
+F32 = mybir.dt.float32
+U32 = mybir.dt.uint32
+U8 = mybir.dt.uint8
+FP8X4 = mybir.dt.float8_e4m3fn_x4
+
+P = 128
+BATCH, STACK, TUBE, IMG, PATCH, EMBED = 4, 16, 2, 256, 64, 512
+GRID = IMG // PATCH
+TUBES = STACK // TUBE
+K = TUBE * PATCH * PATCH
+K_PASS = 4 * P
+PASSES = K // K_PASS
+PASSES_PER_FRAME = PASSES // TUBE
+ROWS_PER_PASS = K_PASS // PATCH
+COL_TILES = 4
+COLUMNS = 2 * EMBED
+
+MULTIPLY_LAG = 2
+POS_AFTER_PASS = 8
+
+FLOPS = 2 * BATCH * TUBES * GRID * GRID * EMBED * K
+
+
+def tile_tubeletembedding_k_kernel(tc, video, W, b, pos_embed, out):
+    nc = tc.nc
+    assert tuple(video.shape) == (BATCH, STACK, 1, IMG, IMG)
+    assert tuple(W.shape) == (EMBED, K)
+    assert BATCH * TUBES * GRID == P
+
+    video_rows = video.rearrange("b (d t) c (i y) x -> t i (b d) (c y x)", t=TUBE, i=GRID)
+    w_rows = W.rearrange("(c p) k -> p c k", p=P)
+    pos_rows = pos_embed.rearrange("o (q j) e -> (o q) (j e)", j=GRID)
+    out_rows = out.rearrange("b (q j) e -> (b q) j e", j=GRID)
+
+    with ExitStack() as ctx:
+        consts = ctx.enter_context(tc.tile_pool(name="consts", bufs=1))
+        loaded = ctx.enter_context(tc.tile_pool(name="loaded", bufs=1))
+        work = ctx.enter_context(tc.tile_pool(name="work", bufs=3))
+        sums = ctx.enter_context(tc.psum_pool(name="sums", bufs=1))
+        banks = ctx.enter_context(tc.psum_pool(name="banks", bufs=4))
+        ctx.enter_context(tc.manual_schedule())
+
+        video_raw = []
+        w_raw = []
+        pos_sb = consts.tile([P, GRID * EMBED], BF16)
+        for g in range(PASSES):
+            ts, y8 = divmod(g, PASSES_PER_FRAME)
+            run = slice(y8 * ROWS_PER_PASS * IMG, (y8 + 1) * ROWS_PER_PASS * IMG)
+            v_in = loaded.tile([P, ROWS_PER_PASS * IMG], BF16, name="v_in%d" % g)
+            for i in range(GRID):
+                nc.sync.dma_start(out=v_in[i:P:GRID, :], in_=video_rows[ts, i, :, run])
+            w_in = loaded.tile([P, COL_TILES * K_PASS], BF16, name="w_in%d" % g)
+            nc.sync.dma_start(
+                out=w_in[:].rearrange("p (c k) -> p c k", c=COL_TILES),
+                in_=w_rows[:, :, g * K_PASS : (g + 1) * K_PASS],
+            )
+            video_raw.append(v_in)
+            w_raw.append(w_in)
+            if g == POS_AFTER_PASS:
+                for batch in range(BATCH):
+                    rows = slice(batch * TUBES * GRID, (batch + 1) * TUBES * GRID)
+                    nc.sync.dma_start(out=pos_sb[rows, :], in_=pos_rows)
+
+        ident = consts.tile([P, P], F32)
+        make_identity(nc, ident[:])
+
+        bias_row = consts.tile([P, EMBED], BF16)
+        nc.vector.memset(bias_row[:], 0.0)
+        nc.scalar.dma_start(out=bias_row[0:1, :], in_=b.rearrange("(o e) -> o e", o=1))
+        ones = consts.tile([P, P], BF16)
+        nc.vector.memset(ones[:], 1.0)
+        bias_bank = banks.tile([P, EMBED], F32, name="bank")
+        nc.tensor.matmul(out=bias_bank[:], lhsT=ones[:], rhs=bias_row[:], start=True, stop=True)
+        bias_all = consts.tile([P, EMBED], F32)
+        nc.scalar.copy(out=bias_all[:], in_=bias_bank[:])
+
+        addend = consts.tile([P, GRID * EMBED], F32)
+        result = consts.tile([P, GRID * EMBED], F32)
+        acc = []
+        for j in range(GRID):
+            acc_j = sums.tile([P, EMBED], F32, name="acc%d" % j)
+            acc.append(acc_j)
+
+        video_tok = {}
+        grouped = {}
+        codes = {}
+        scales = {}
+
+        def regroup(g):
+            v_tok = work.tile([P, COL_TILES * K_PASS], BF16, name="v_tok")
+            to = v_tok[:].bitcast(F32).rearrange("p (j u y x) -> p u j y x", j=GRID, u=2, x=PATCH // 4)
+            frm = video_raw[g][:].bitcast(F32).rearrange("p (y j x u) -> p u j y x", j=GRID, u=2, x=PATCH // 4)
+            for u in range(2):
+                nc.vector.tensor_copy(out=to[:, u], in_=frm[:, u])
+            video_tok[g] = v_tok
+
+        def transpose_and_group(source, target_words, split):
+            words = source[:].bitcast(F32)
+            for pair in range(COL_TILES // 2):
+                bank = banks.tile([P, 2, 2 * P], F32, name="bank")
+                for c in range(2):
+                    for u in range(2):
+                        run = (2 * pair + c) * 2 * P
+                        if split:
+                            picked = slice(run + u * P, run + (u + 1) * P)
+                        else:
+                            picked = slice(run + u, run + 2 * P, 2)
+                        nc.tensor.transpose(
+                            bank[:, u, c * P : (c + 1) * P], words[:, picked], ident[:]
+                        )
+                nc.scalar.copy(
+                    out=target_words[:, pair * 2 * P : (pair + 1) * 2 * P, :],
+                    in_=bank[:].rearrange("p u c -> p c u"),
+                )
+
+        def transpose(g):
+            grp = work.tile([P, COLUMNS * 4], BF16, name="grp", align_bytes=64)
+            grp_words = grp[:].bitcast(F32).rearrange("p (c u) -> p c u", u=2)
+            transpose_and_group(video_tok[g], grp_words[:, EMBED:COLUMNS, :], True)
+            transpose_and_group(w_raw[g], grp_words[:, 0:EMBED, :], False)
+            grouped[g] = grp
+
+        def quantise(g):
+            cod = work.tile([P, COLUMNS], U32, name="cod", align_bytes=64)
+            sca = work.tile([P, COLUMNS], U8, name="sca", align_bytes=64)
+            nc.vector.quantize_mx(out=cod[:].bitcast(FP8X4), scales=sca[:], in_=grouped[g][:])
+            codes[g] = cod
+            scales[g] = sca
+
+        def multiply(g):
+            for j in range(GRID):
+                tokens = slice(EMBED + j * P, EMBED + (j + 1) * P)
+                nc.tensor.matmul_mx(
+                    out=acc[j][:],
+                    lhsT=codes[g][:, tokens].bitcast(FP8X4),
+                    lhsT_scale=scales[g][:, tokens],
+                    rhs=codes[g][:, 0:EMBED].bitcast(FP8X4),
+                    rhs_scale=scales[g][:, 0:EMBED],
+                    start=(g == 0),
+                    stop=(g == PASSES - 1),
+                )
+
+        regroup(0)
+        for s in range(PASSES + MULTIPLY_LAG):
+            if s < PASSES:
+                transpose(s)
+            if 1 <= s <= PASSES:
+                quantise(s - 1)
+            if s >= MULTIPLY_LAG:
+                multiply(s - MULTIPLY_LAG)
+            if s + 1 < PASSES:
+                regroup(s + 1)
+            j = s - (POS_AFTER_PASS + 2)
+            if 0 <= j < GRID:
+                part = slice(j * EMBED, (j + 1) * EMBED)
+                nc.vector.tensor_tensor(
+                    out=addend[:, part], in0=pos_sb[:, part], in1=bias_all[:], op=mybir.AluOpType.add
+                )
+
+        for j in range(GRID):
+            part = slice(j * EMBED, (j + 1) * EMBED)
+            nc.vector.tensor_tensor(
+                out=result[:, part], in0=acc[j][:], in1=addend[:, part], op=mybir.AluOpType.add
+            )
+            nc.sync.dma_start(out=out_rows[:, j, :], in_=result[:, part])

@@ -14,26 +14,22 @@ BATCH, STACK, TUBE, IMG, PATCH, EMBED = 4, 16, 2, 256, 64, 512
 GRID = IMG // PATCH
 TUBES = STACK // TUBE
 K = TUBE * PATCH * PATCH
+K_FRAME = PATCH * PATCH
 K_PASS = 4 * P
-PASSES = K // K_PASS
-PASSES_PER_FRAME = PASSES // TUBE
-ROWS_PER_PASS = K_PASS // PATCH
-COL_TILES = 4
+BANDS = K_FRAME // K_PASS
+BAND_ROWS = PATCH // BANDS
+BAND_WORDS = BAND_ROWS * IMG // 2
+HALVES = 2
+HALF_TOK = P // TUBE
 COLUMNS = 2 * EMBED
-
-MULTIPLY_LAG = 2
-POS_AFTER_PASS = 8
+Q = TUBES * GRID
 
 FLOPS = 2 * BATCH * TUBES * GRID * GRID * EMBED * K
 
 
 def tile_tubeletembedding_k_kernel(tc, video, W, b, pos_embed, out):
     nc = tc.nc
-    assert tuple(video.shape) == (BATCH, STACK, 1, IMG, IMG)
-    assert tuple(W.shape) == (EMBED, K)
-    assert BATCH * TUBES * GRID == P
-
-    video_rows = video.rearrange("b (d t) c (i y) x -> t i (b d) (c y x)", t=TUBE, i=GRID)
+    video_rows = video.rearrange("b s c (i y) x -> (b s i) (c y x)", i=GRID)
     w_rows = W.rearrange("(c p) k -> p c k", p=P)
     pos_rows = pos_embed.rearrange("o (q j) e -> (o q) (j e)", j=GRID)
     out_rows = out.rearrange("b (q j) e -> (b q) j e", j=GRID)
@@ -41,44 +37,63 @@ def tile_tubeletembedding_k_kernel(tc, video, W, b, pos_embed, out):
     with ExitStack() as ctx:
         consts = ctx.enter_context(tc.tile_pool(name="consts", bufs=1))
         loaded = ctx.enter_context(tc.tile_pool(name="loaded", bufs=1))
-        work = ctx.enter_context(tc.tile_pool(name="work", bufs=3))
+        regrouped = ctx.enter_context(tc.tile_pool(name="regrouped", bufs=2))
+        work = ctx.enter_context(tc.tile_pool(name="work", bufs=2))
         sums = ctx.enter_context(tc.psum_pool(name="sums", bufs=1))
         banks = ctx.enter_context(tc.psum_pool(name="banks", bufs=4))
         ctx.enter_context(tc.manual_schedule())
 
-        video_raw = []
-        w_raw = []
+        v_raw = {}
+        w_src = {}
         pos_sb = consts.tile([P, GRID * EMBED], BF16)
-        for g in range(PASSES):
-            ts, y8 = divmod(g, PASSES_PER_FRAME)
-            run = slice(y8 * ROWS_PER_PASS * IMG, (y8 + 1) * ROWS_PER_PASS * IMG)
-            v_in = loaded.tile([P, ROWS_PER_PASS * IMG], BF16, name="v_in%d" % g)
-            for i in range(GRID):
-                nc.sync.dma_start(out=v_in[i:P:GRID, :], in_=video_rows[ts, i, :, run])
-            w_in = loaded.tile([P, COL_TILES * K_PASS], BF16, name="w_in%d" % g)
-            nc.sync.dma_start(
-                out=w_in[:].rearrange("p (c k) -> p c k", c=COL_TILES),
-                in_=w_rows[:, :, g * K_PASS : (g + 1) * K_PASS],
-            )
-            video_raw.append(v_in)
-            w_raw.append(w_in)
-            if g == POS_AFTER_PASS:
-                for batch in range(BATCH):
-                    rows = slice(batch * TUBES * GRID, (batch + 1) * TUBES * GRID)
-                    nc.sync.dma_start(out=pos_sb[rows, :], in_=pos_rows)
+        nc.gpsimd.memset(pos_sb[:], 0.0)
+
+        def load_video(t):
+            run = slice(t * BAND_ROWS * IMG, (t + 1) * BAND_ROWS * IMG)
+            for h in range(HALVES):
+                v_in = loaded.tile([P, BAND_ROWS * IMG], BF16, name="v_in%d_%d" % (t, h))
+                nc.sync.dma_start(out=v_in[:], in_=video_rows[h * P : (h + 1) * P, run])
+                v_raw[t, h] = v_in
+
+        def load_w(ts, t, bands):
+            width = bands * K_PASS
+            first = ts * K_FRAME + t * K_PASS
+            w_in = loaded.tile([P, GRID * width], BF16, name="w_in%d_%d" % (t, ts))
+            view = w_in[:].rearrange("p (c k) -> p c k", c=GRID)
+            nc.sync.dma_start(out=view, in_=w_rows[:, :, first : first + width])
+            for n in range(bands):
+                w_src[t + n, ts] = (w_in, width, n * K_PASS)
+
+        load_w(0, 0, 1)
+        load_video(0)
+        load_w(1, 0, 1)
+        load_video(1)
+        load_w(0, 1, 1)
+        load_w(1, 1, 1)
+        for t in range(2, BANDS, 2):
+            load_video(t)
+            load_w(0, t, 2)
+            load_w(1, t, 2)
+            load_video(t + 1)
+            if t == 2:
+                nc.sync.dma_start(out=pos_sb[0:Q, :], in_=pos_rows)
+                for j in range(GRID):
+                    nc.sync.dma_start(
+                        out=pos_sb[Q : Q + 1, j * EMBED : (j + 1) * EMBED],
+                        in_=b.rearrange("(o e) -> o e", o=1),
+                    )
 
         ident = consts.tile([P, P], F32)
         make_identity(nc, ident[:])
-
-        bias_row = consts.tile([P, EMBED], BF16)
-        nc.vector.memset(bias_row[:], 0.0)
-        nc.scalar.dma_start(out=bias_row[0:1, :], in_=b.rearrange("(o e) -> o e", o=1))
-        ones = consts.tile([P, P], BF16)
-        nc.vector.memset(ones[:], 1.0)
-        bias_bank = banks.tile([P, EMBED], F32, name="bank")
-        nc.tensor.matmul(out=bias_bank[:], lhsT=ones[:], rhs=bias_row[:], start=True, stop=True)
-        bias_all = consts.tile([P, EMBED], F32)
-        nc.scalar.copy(out=bias_all[:], in_=bias_bank[:])
+        perm = consts.tile([P, P], F32)
+        nc.vector.tensor_copy(
+            out=perm[:].rearrange("p (f n i) -> p n f i", f=TUBE, i=GRID),
+            in_=ident[:].rearrange("p (n f i) -> p n f i", f=TUBE, i=GRID),
+        )
+        select = consts.tile([P, P], BF16)
+        for batch in range(BATCH):
+            nc.vector.tensor_copy(out=select[:, batch * Q : (batch + 1) * Q], in_=ident[:, 0:Q])
+        nc.vector.memset(select[Q : Q + 1, :], 1.0)
 
         addend = consts.tile([P, GRID * EMBED], F32)
         result = consts.tile([P, GRID * EMBED], F32)
@@ -87,83 +102,114 @@ def tile_tubeletembedding_k_kernel(tc, video, W, b, pos_embed, out):
             acc_j = sums.tile([P, EMBED], F32, name="acc%d" % j)
             acc.append(acc_j)
 
-        video_tok = {}
+        v_tok = {}
         grouped = {}
         codes = {}
         scales = {}
 
-        def regroup(g):
-            v_tok = work.tile([P, COL_TILES * K_PASS], BF16, name="v_tok")
-            to = v_tok[:].bitcast(F32).rearrange("p (j u y x) -> p u j y x", j=GRID, u=2, x=PATCH // 4)
-            frm = video_raw[g][:].bitcast(F32).rearrange("p (y j x u) -> p u j y x", j=GRID, u=2, x=PATCH // 4)
-            for u in range(2):
-                nc.vector.tensor_copy(out=to[:, u], in_=frm[:, u])
-            video_tok[g] = v_tok
+        def regroup(t, h):
+            tok = regrouped.tile([P, BAND_ROWS * IMG], BF16, name="tok%d" % h)
+            nc.vector.tensor_copy(
+                out=tok[:].bitcast(F32).rearrange("p (j u y x) -> p j u y x", j=GRID, u=2, y=BAND_ROWS),
+                in_=v_raw[t, h][:].bitcast(F32).rearrange("p (y j x u) -> p j u y x", j=GRID, u=2, y=BAND_ROWS),
+            )
+            v_tok[t, h] = tok
 
-        def transpose_and_group(source, target_words, split):
-            words = source[:].bitcast(F32)
-            for pair in range(COL_TILES // 2):
+        def transpose_video(t, j):
+            bank = banks.tile([P, 2, TUBE, P], F32, name="bank")
+            for h in range(HALVES):
+                words = v_tok[t, h][:].bitcast(F32)
+                for u in range(2):
+                    first = (j * 2 + u) * P
+                    nc.tensor.transpose(
+                        bank[:, u, :, h * HALF_TOK : (h + 1) * HALF_TOK], words[:, first : first + P], perm[:]
+                    )
+            grp = grouped[t][:].bitcast(F32).rearrange("p (f c u) -> p f c u", f=TUBE, u=2)
+            first = EMBED + j * P
+            nc.scalar.copy(
+                out=grp[:, :, first : first + P, :],
+                in_=bank[:].rearrange("p u f c -> p f c u"),
+            )
+
+        def transpose_w(t, ts):
+            w_in, width, offset = w_src[t, ts]
+            words = w_in[:].bitcast(F32)
+            grp = grouped[t][:].bitcast(F32).rearrange("p (f c u) -> p f c u", f=TUBE, u=2)
+            for pair in range(2):
                 bank = banks.tile([P, 2, 2 * P], F32, name="bank")
                 for c in range(2):
+                    first = ((2 * pair + c) * width + offset) // 2
                     for u in range(2):
-                        run = (2 * pair + c) * 2 * P
-                        if split:
-                            picked = slice(run + u * P, run + (u + 1) * P)
-                        else:
-                            picked = slice(run + u, run + 2 * P, 2)
                         nc.tensor.transpose(
-                            bank[:, u, c * P : (c + 1) * P], words[:, picked], ident[:]
+                            bank[:, u, c * P : (c + 1) * P], words[:, first + u : first + 2 * P : 2], ident[:]
                         )
                 nc.scalar.copy(
-                    out=target_words[:, pair * 2 * P : (pair + 1) * 2 * P, :],
+                    out=grp[:, ts, pair * 2 * P : (pair + 1) * 2 * P, :],
                     in_=bank[:].rearrange("p u c -> p c u"),
                 )
 
-        def transpose(g):
-            grp = work.tile([P, COLUMNS * 4], BF16, name="grp", align_bytes=64)
-            grp_words = grp[:].bitcast(F32).rearrange("p (c u) -> p c u", u=2)
-            transpose_and_group(video_tok[g], grp_words[:, EMBED:COLUMNS, :], True)
-            transpose_and_group(w_raw[g], grp_words[:, 0:EMBED, :], False)
-            grouped[g] = grp
+        def quantise(t, ts, first=0, last=COLUMNS):
+            if (t, ts) not in codes:
+                cod = work.tile([P, COLUMNS], U32, name="cod%d" % ts, align_bytes=64)
+                sca = work.tile([P, COLUMNS], U8, name="sca%d" % ts, align_bytes=64)
+                codes[t, ts] = cod
+                scales[t, ts] = sca
+            nc.vector.quantize_mx(
+                out=codes[t, ts][:, first:last].bitcast(FP8X4),
+                scales=scales[t, ts][:, first:last],
+                in_=grouped[t][:, (ts * COLUMNS + first) * 4 : (ts * COLUMNS + last) * 4],
+            )
 
-        def quantise(g):
-            cod = work.tile([P, COLUMNS], U32, name="cod", align_bytes=64)
-            sca = work.tile([P, COLUMNS], U8, name="sca", align_bytes=64)
-            nc.vector.quantize_mx(out=cod[:].bitcast(FP8X4), scales=sca[:], in_=grouped[g][:])
-            codes[g] = cod
-            scales[g] = sca
+        def multiply(t, ts, j):
+            tokens = slice(EMBED + j * P, EMBED + (j + 1) * P)
+            nc.tensor.matmul_mx(
+                out=acc[j][:],
+                lhsT=codes[t, ts][:, tokens].bitcast(FP8X4),
+                lhsT_scale=scales[t, ts][:, tokens],
+                rhs=codes[t, ts][:, 0:EMBED].bitcast(FP8X4),
+                rhs_scale=scales[t, ts][:, 0:EMBED],
+                start=(t == 0 and ts == 0),
+                stop=(t == BANDS - 1 and ts == TUBE - 1),
+            )
 
-        def multiply(g):
-            for j in range(GRID):
-                tokens = slice(EMBED + j * P, EMBED + (j + 1) * P)
-                nc.tensor.matmul_mx(
-                    out=acc[j][:],
-                    lhsT=codes[g][:, tokens].bitcast(FP8X4),
-                    lhsT_scale=scales[g][:, tokens],
-                    rhs=codes[g][:, 0:EMBED].bitcast(FP8X4),
-                    rhs_scale=scales[g][:, 0:EMBED],
-                    start=(g == 0),
-                    stop=(g == PASSES - 1),
-                )
+        def add_bias(j):
+            part = slice(j * EMBED, (j + 1) * EMBED)
+            bank = banks.tile([P, EMBED], F32, name="bank")
+            nc.tensor.matmul(out=bank[:], lhsT=select[:], rhs=pos_sb[:, part], start=True, stop=True)
+            nc.vector.tensor_copy(out=addend[:, part], in_=bank[:])
 
-        regroup(0)
-        for s in range(PASSES + MULTIPLY_LAG):
-            if s < PASSES:
-                transpose(s)
-            if 1 <= s <= PASSES:
-                quantise(s - 1)
-            if s >= MULTIPLY_LAG:
-                multiply(s - MULTIPLY_LAG)
-            if s + 1 < PASSES:
-                regroup(s + 1)
-            j = s - (POS_AFTER_PASS + 2)
-            if 0 <= j < GRID:
-                part = slice(j * EMBED, (j + 1) * EMBED)
-                nc.vector.tensor_tensor(
-                    out=addend[:, part], in0=pos_sb[:, part], in1=bias_all[:], op=mybir.AluOpType.add
-                )
+        for h in range(HALVES):
+            regroup(0, h)
+        for t in range(BANDS):
+            grp_t = work.tile([P, TUBE * 4 * 2 * EMBED], BF16, name="grp", align_bytes=64)
+            grouped[t] = grp_t
+            for ts in range(TUBE):
+                if t < BANDS - 1:
+                    transpose_w(t, ts)
+                    for j in range(2 * ts, 2 * ts + 2):
+                        transpose_video(t, j)
+                elif ts == 0:
+                    for j in range(GRID):
+                        transpose_video(t, j)
+                else:
+                    for frame in range(TUBE):
+                        transpose_w(t, frame)
+                if t >= 1:
+                    quantise(t - 1, ts)
+                    for j in range(GRID):
+                        multiply(t - 1, ts, j)
+                if t + 1 < BANDS:
+                    regroup(t + 1, ts)
+            if 3 <= t < 3 + GRID:
+                add_bias(t - 3)
 
+        for first, last in ((EMBED, COLUMNS), (0, EMBED)):
+            for ts in range(TUBE):
+                quantise(BANDS - 1, ts, first, last)
         for j in range(GRID):
+            multiply(BANDS - 1, 0, j)
+        for j in range(GRID):
+            multiply(BANDS - 1, 1, j)
             part = slice(j * EMBED, (j + 1) * EMBED)
             nc.vector.tensor_tensor(
                 out=result[:, part], in0=acc[j][:], in1=addend[:, part], op=mybir.AluOpType.add

@@ -70,18 +70,16 @@ def tile_tubeletembedding_k_kernel(tc, video, W, b, pos_embed, out):
         load_video(1)
         load_w(0, 1, 1)
         load_w(1, 1, 1)
+        nc.scalar.dma_start(out=pos_sb[0:Q, :], in_=pos_rows)
+        for j in range(GRID):
+            nc.scalar.dma_start(
+                out=pos_sb[Q : Q + 1, j * EMBED : (j + 1) * EMBED], in_=b.rearrange("(o e) -> o e", o=1)
+            )
         for t in range(2, BANDS, 2):
             load_video(t)
             load_w(0, t, 2)
             load_w(1, t, 2)
             load_video(t + 1)
-            if t == 2:
-                nc.sync.dma_start(out=pos_sb[0:Q, :], in_=pos_rows)
-                for j in range(GRID):
-                    nc.sync.dma_start(
-                        out=pos_sb[Q : Q + 1, j * EMBED : (j + 1) * EMBED],
-                        in_=b.rearrange("(o e) -> o e", o=1),
-                    )
 
         ident = consts.tile([P, P], F32)
         make_identity(nc, ident[:])
@@ -96,13 +94,13 @@ def tile_tubeletembedding_k_kernel(tc, video, W, b, pos_embed, out):
         nc.vector.memset(select[Q : Q + 1, :], 1.0)
 
         addend = consts.tile([P, GRID * EMBED], F32)
-        result = consts.tile([P, GRID * EMBED], F32)
         acc = []
         for j in range(GRID):
             acc_j = sums.tile([P, EMBED], F32, name="acc%d" % j)
             acc.append(acc_j)
 
         v_tok = {}
+        w_tok = {}
         grouped = {}
         codes = {}
         scales = {}
@@ -114,6 +112,17 @@ def tile_tubeletembedding_k_kernel(tc, video, W, b, pos_embed, out):
                 in_=v_raw[t, h][:].bitcast(F32).rearrange("p (y j x u) -> p j u y x", j=GRID, u=2, y=BAND_ROWS),
             )
             v_tok[t, h] = tok
+
+        def regroup_w(t, ts):
+            w_in, width, offset = w_src[t, ts]
+            tok = regrouped.tile([P, GRID * K_PASS], BF16, name="w_tok%d" % ts)
+            view = w_in[:].bitcast(F32).rearrange("p (c w) -> p c w", c=GRID)
+            first = offset // 2
+            nc.vector.tensor_copy(
+                out=tok[:].bitcast(F32).rearrange("p (c u w) -> p c u w", c=GRID, u=2),
+                in_=view[:, :, first : first + 2 * P].rearrange("p c (w u) -> p c u w", u=2),
+            )
+            w_tok[t, ts] = tok
 
         def transpose_video(t, j):
             bank = banks.tile([P, 2, TUBE, P], F32, name="bank")
@@ -132,16 +141,15 @@ def tile_tubeletembedding_k_kernel(tc, video, W, b, pos_embed, out):
             )
 
         def transpose_w(t, ts):
-            w_in, width, offset = w_src[t, ts]
-            words = w_in[:].bitcast(F32)
+            words = w_tok[t, ts][:].bitcast(F32)
             grp = grouped[t][:].bitcast(F32).rearrange("p (f c u) -> p f c u", f=TUBE, u=2)
             for pair in range(2):
                 bank = banks.tile([P, 2, 2 * P], F32, name="bank")
                 for c in range(2):
-                    first = ((2 * pair + c) * width + offset) // 2
                     for u in range(2):
+                        first = ((2 * pair + c) * 2 + u) * P
                         nc.tensor.transpose(
-                            bank[:, u, c * P : (c + 1) * P], words[:, first + u : first + 2 * P : 2], ident[:]
+                            bank[:, u, c * P : (c + 1) * P], words[:, first : first + P], ident[:]
                         )
                 nc.scalar.copy(
                     out=grp[:, ts, pair * 2 * P : (pair + 1) * 2 * P, :],
@@ -176,42 +184,53 @@ def tile_tubeletembedding_k_kernel(tc, video, W, b, pos_embed, out):
             part = slice(j * EMBED, (j + 1) * EMBED)
             bank = banks.tile([P, EMBED], F32, name="bank")
             nc.tensor.matmul(out=bank[:], lhsT=select[:], rhs=pos_sb[:, part], start=True, stop=True)
-            nc.vector.tensor_copy(out=addend[:, part], in_=bank[:])
+            nc.scalar.copy(out=addend[:, part], in_=bank[:])
 
+        WEIGHTS, TOKENS = (0, EMBED), (EMBED, COLUMNS)
+
+        def multiply_pass(t, ts):
+            for j in range(GRID):
+                multiply(t, ts, j)
+
+        regroup_w(0, 0)
         for h in range(HALVES):
             regroup(0, h)
+        regroup_w(0, 1)
         for t in range(BANDS):
-            grp_t = work.tile([P, TUBE * 4 * 2 * EMBED], BF16, name="grp", align_bytes=64)
+            grp_t = work.tile([P, TUBE * 4 * COLUMNS], BF16, name="grp", align_bytes=64)
             grouped[t] = grp_t
-            for ts in range(TUBE):
-                if t < BANDS - 1:
-                    transpose_w(t, ts)
-                    for j in range(2 * ts, 2 * ts + 2):
-                        transpose_video(t, j)
-                elif ts == 0:
-                    for j in range(GRID):
-                        transpose_video(t, j)
-                else:
-                    for frame in range(TUBE):
-                        transpose_w(t, frame)
-                if t >= 1:
-                    quantise(t - 1, ts)
-                    for j in range(GRID):
-                        multiply(t - 1, ts, j)
-                if t + 1 < BANDS:
-                    regroup(t + 1, ts)
-            if 3 <= t < 3 + GRID:
-                add_bias(t - 3)
+            transpose_w(t, 0)
+            transpose_video(t, 0)
+            transpose_video(t, 1)
+            if t >= 1:
+                quantise(t - 1, 0, *TOKENS)
+                quantise(t - 1, 1, *TOKENS)
+                quantise(t - 1, 1, *WEIGHTS)
+                multiply_pass(t - 1, 0)
+            if t + 1 < BANDS:
+                for h in range(HALVES):
+                    regroup(t + 1, h)
+            quantise(t, 0, *WEIGHTS)
+            transpose_video(t, 2)
+            transpose_video(t, 3)
+            transpose_w(t, 1)
+            if t >= 1:
+                multiply_pass(t - 1, 1)
+            if t + 1 < BANDS:
+                for ts in range(TUBE):
+                    regroup_w(t + 1, ts)
+            if t == 0:
+                for j in range(GRID):
+                    add_bias(j)
 
-        for first, last in ((EMBED, COLUMNS), (0, EMBED)):
-            for ts in range(TUBE):
-                quantise(BANDS - 1, ts, first, last)
-        for j in range(GRID):
-            multiply(BANDS - 1, 0, j)
+        quantise(BANDS - 1, 0, *TOKENS)
+        multiply_pass(BANDS - 1, 0)
+        quantise(BANDS - 1, 1, *TOKENS)
+        quantise(BANDS - 1, 1, *WEIGHTS)
         for j in range(GRID):
             multiply(BANDS - 1, 1, j)
             part = slice(j * EMBED, (j + 1) * EMBED)
             nc.vector.tensor_tensor(
-                out=result[:, part], in0=acc[j][:], in1=addend[:, part], op=mybir.AluOpType.add
+                out=addend[:, part], in0=acc[j][:], in1=addend[:, part], op=mybir.AluOpType.add
             )
-            nc.sync.dma_start(out=out_rows[:, j, :], in_=result[:, part])
+            nc.sync.dma_start(out=out_rows[:, j, :], in_=addend[:, part])

@@ -46,7 +46,15 @@ def tile_tubeletembedding_k_kernel(tc, video, W, b, pos_embed, out):
         v_raw = {}
         w_src = {}
         pos_sb = consts.tile([P, GRID * EMBED], BF16)
-        nc.gpsimd.memset(pos_sb[:], 0.0)
+        nc.vector.memset(pos_sb[:].bitcast(F32), 0.0)
+        warm = consts.tile([P, 1], F32)
+        nc.vector.memset(warm[:], 0.0)
+        nc.scalar.copy(out=warm[:], in_=warm[:])
+        nc.scalar.dma_start(out=pos_sb[0:Q, :], in_=pos_rows)
+        nc.scalar.dma_start(
+            out=pos_sb[Q : Q + 1, :].rearrange("p (j e) -> p j e", j=GRID),
+            in_=b.rearrange("(o j e) -> o j e", o=1, j=1).to_broadcast([1, GRID, EMBED]),
+        )
 
         def load_video(t):
             run = slice(t * BAND_ROWS * IMG, (t + 1) * BAND_ROWS * IMG)
@@ -70,12 +78,11 @@ def tile_tubeletembedding_k_kernel(tc, video, W, b, pos_embed, out):
         load_video(1)
         load_w(0, 1, 1)
         load_w(1, 1, 1)
-        nc.scalar.dma_start(out=pos_sb[0:Q, :], in_=pos_rows)
-        for j in range(GRID):
-            nc.scalar.dma_start(
-                out=pos_sb[Q : Q + 1, j * EMBED : (j + 1) * EMBED], in_=b.rearrange("(o e) -> o e", o=1)
-            )
-        for t in range(2, BANDS, 2):
+        for t in range(2, 4):
+            load_video(t)
+            load_w(0, t, 1)
+            load_w(1, t, 1)
+        for t in range(4, BANDS, 2):
             load_video(t)
             load_w(0, t, 2)
             load_w(1, t, 2)

@@ -18,10 +18,11 @@ K_FRAME = PATCH * PATCH
 K_PASS = 4 * P
 BANDS = K_FRAME // K_PASS
 BAND_ROWS = PATCH // BANDS
-BAND_WORDS = BAND_ROWS * IMG // 2
+BAND_ROW_PIXELS = BAND_ROWS * IMG
 HALVES = 2
-HALF_TOK = P // TUBE
-COLUMNS = 2 * EMBED
+PAIRS = 2
+PAIR_TOK = P // 2
+COLUMNS = 512
 Q = TUBES * GRID
 
 FLOPS = 2 * BATCH * TUBES * GRID * GRID * EMBED * K
@@ -37,14 +38,11 @@ def tile_tubeletembedding_k_kernel(tc, video, W, b, pos_embed, out):
     with ExitStack() as ctx:
         consts = ctx.enter_context(tc.tile_pool(name="consts", bufs=1))
         loaded = ctx.enter_context(tc.tile_pool(name="loaded", bufs=1))
-        regrouped = ctx.enter_context(tc.tile_pool(name="regrouped", bufs=2))
-        work = ctx.enter_context(tc.tile_pool(name="work", bufs=2))
+        work = ctx.enter_context(tc.tile_pool(name="work", bufs=3))
         sums = ctx.enter_context(tc.psum_pool(name="sums", bufs=1))
         banks = ctx.enter_context(tc.psum_pool(name="banks", bufs=4))
         ctx.enter_context(tc.manual_schedule())
 
-        v_raw = {}
-        w_src = {}
         pos_sb = consts.tile([P, GRID * EMBED], BF16)
         nc.vector.memset(pos_sb[:].bitcast(F32), 0.0)
         warm = consts.tile([P, 1], F32)
@@ -55,38 +53,26 @@ def tile_tubeletembedding_k_kernel(tc, video, W, b, pos_embed, out):
             out=pos_sb[Q : Q + 1, :].rearrange("p (j e) -> p j e", j=GRID),
             in_=b.rearrange("(o j e) -> o j e", o=1, j=1).to_broadcast([1, GRID, EMBED]),
         )
+        v_raw = {}
+        w_raw = {}
 
-        def load_video(t):
-            run = slice(t * BAND_ROWS * IMG, (t + 1) * BAND_ROWS * IMG)
-            for h in range(HALVES):
-                v_in = loaded.tile([P, BAND_ROWS * IMG], BF16, name="v_in%d_%d" % (t, h))
-                nc.sync.dma_start(out=v_in[:], in_=video_rows[h * P : (h + 1) * P, run])
-                v_raw[t, h] = v_in
+        def load_video(t, h):
+            v_in = loaded.tile([P, BAND_ROW_PIXELS], BF16, name="v_in%d_%d" % (t, h))
+            run = slice(t * BAND_ROW_PIXELS, (t + 1) * BAND_ROW_PIXELS)
+            nc.sync.dma_start(out=v_in[:], in_=video_rows[h * P : (h + 1) * P, run])
+            v_raw[t, h] = v_in
 
-        def load_w(ts, t, bands):
-            width = bands * K_PASS
+        def load_w(t, ts):
             first = ts * K_FRAME + t * K_PASS
-            w_in = loaded.tile([P, GRID * width], BF16, name="w_in%d_%d" % (t, ts))
+            w_in = loaded.tile([P, GRID * K_PASS], BF16, name="w_in%d_%d" % (t, ts))
             view = w_in[:].rearrange("p (c k) -> p c k", c=GRID)
-            nc.sync.dma_start(out=view, in_=w_rows[:, :, first : first + width])
-            for n in range(bands):
-                w_src[t + n, ts] = (w_in, width, n * K_PASS)
+            nc.sync.dma_start(out=view, in_=w_rows[:, :, first : first + K_PASS])
+            w_raw[t, ts] = w_in
 
-        load_w(0, 0, 1)
-        load_video(0)
-        load_w(1, 0, 1)
-        load_video(1)
-        load_w(0, 1, 1)
-        load_w(1, 1, 1)
-        for t in range(2, 4):
-            load_video(t)
-            load_w(0, t, 1)
-            load_w(1, t, 1)
-        for t in range(4, BANDS, 2):
-            load_video(t)
-            load_w(0, t, 2)
-            load_w(1, t, 2)
-            load_video(t + 1)
+        for t in range(BANDS):
+            for n in range(2):
+                load_w(t, n)
+                load_video(t, n)
 
         ident = consts.tile([P, P], F32)
         make_identity(nc, ident[:])
@@ -95,25 +81,29 @@ def tile_tubeletembedding_k_kernel(tc, video, W, b, pos_embed, out):
             out=perm[:].rearrange("p (f n i) -> p n f i", f=TUBE, i=GRID),
             in_=ident[:].rearrange("p (n f i) -> p n f i", f=TUBE, i=GRID),
         )
-        select = consts.tile([P, P], BF16)
-        for batch in range(BATCH):
-            nc.vector.tensor_copy(out=select[:, batch * Q : (batch + 1) * Q], in_=ident[:, 0:Q])
-        nc.vector.memset(select[Q : Q + 1, :], 1.0)
+        select = consts.tile([P, 3 * PAIR_TOK], BF16)
+        nc.vector.memset(select[:], 0.0)
+        for batch in range(2):
+            first = PAIR_TOK + batch * Q
+            nc.vector.tensor_copy(out=select[:, first : first + Q], in_=ident[:, 0:Q])
+        nc.vector.memset(select[Q : Q + 1, PAIR_TOK : 2 * PAIR_TOK], 1.0)
 
-        addend = consts.tile([P, GRID * EMBED], F32)
-        acc = []
-        for j in range(GRID):
-            acc_j = sums.tile([P, EMBED], F32, name="acc%d" % j)
-            acc.append(acc_j)
+        addend = consts.tile([P, PAIRS * EMBED], F32)
+        acc = {}
+        for h in range(HALVES):
+            for pair in range(PAIRS):
+                acc_q = sums.tile([P, EMBED], F32, name="acc%d_%d" % (h, pair))
+                acc[h, pair] = acc_q
 
         v_tok = {}
         w_tok = {}
-        grouped = {}
-        codes = {}
-        scales = {}
+        v_grp = {}
+        w_grp = {}
+        v_mx = {}
+        w_mx = {}
 
-        def regroup(t, h):
-            tok = regrouped.tile([P, BAND_ROWS * IMG], BF16, name="tok%d" % h)
+        def regroup_video(t, h):
+            tok = work.tile([P, BAND_ROW_PIXELS], BF16, name="v_tok")
             nc.vector.tensor_copy(
                 out=tok[:].bitcast(F32).rearrange("p (j u y x) -> p j u y x", j=GRID, u=2, y=BAND_ROWS),
                 in_=v_raw[t, h][:].bitcast(F32).rearrange("p (y j x u) -> p j u y x", j=GRID, u=2, y=BAND_ROWS),
@@ -121,123 +111,148 @@ def tile_tubeletembedding_k_kernel(tc, video, W, b, pos_embed, out):
             v_tok[t, h] = tok
 
         def regroup_w(t, ts):
-            w_in, width, offset = w_src[t, ts]
-            tok = regrouped.tile([P, GRID * K_PASS], BF16, name="w_tok%d" % ts)
-            view = w_in[:].bitcast(F32).rearrange("p (c w) -> p c w", c=GRID)
-            first = offset // 2
+            tok = work.tile([P, GRID * K_PASS], BF16, name="w_tok")
             nc.vector.tensor_copy(
                 out=tok[:].bitcast(F32).rearrange("p (c u w) -> p c u w", c=GRID, u=2),
-                in_=view[:, :, first : first + 2 * P].rearrange("p c (w u) -> p c u w", u=2),
+                in_=w_raw[t, ts][:].bitcast(F32).rearrange("p (c w u) -> p c u w", c=GRID, u=2),
             )
             w_tok[t, ts] = tok
 
-        def transpose_video(t, j):
-            bank = banks.tile([P, 2, TUBE, P], F32, name="bank")
-            for h in range(HALVES):
-                words = v_tok[t, h][:].bitcast(F32)
-                for u in range(2):
-                    first = (j * 2 + u) * P
-                    nc.tensor.transpose(
-                        bank[:, u, :, h * HALF_TOK : (h + 1) * HALF_TOK], words[:, first : first + P], perm[:]
-                    )
-            grp = grouped[t][:].bitcast(F32).rearrange("p (f c u) -> p f c u", f=TUBE, u=2)
-            first = EMBED + j * P
-            nc.scalar.copy(
-                out=grp[:, :, first : first + P, :],
-                in_=bank[:].rearrange("p u f c -> p f c u"),
-            )
+        def transpose_video(t, h):
+            grp = work.tile([P, 4 * COLUMNS], BF16, name="v_grp", align_bytes=64)
+            target = grp[:].bitcast(F32).rearrange("p (j f c u) -> p j f c u", f=TUBE, j=PAIRS, u=2)
+            words = v_tok[t, h][:].bitcast(F32)
+            for pair in range(PAIRS):
+                bank = banks.tile([P, 2, TUBE, P], F32, name="bank")
+                for n in range(2):
+                    for u in range(2):
+                        first = ((2 * pair + n) * 2 + u) * P
+                        nc.tensor.transpose(
+                            bank[:, u, :, n * PAIR_TOK : (n + 1) * PAIR_TOK], words[:, first : first + P], perm[:]
+                        )
+                nc.scalar.copy(out=target[:, pair], in_=bank[:].rearrange("p u f c -> p f c u"))
+            v_grp[t, h] = grp
 
         def transpose_w(t, ts):
+            grp = work.tile([P, 4 * COLUMNS], BF16, name="w_grp", align_bytes=64)
+            target = grp[:].bitcast(F32).rearrange("p (n c u) -> p n c u", n=2, u=2)
             words = w_tok[t, ts][:].bitcast(F32)
-            grp = grouped[t][:].bitcast(F32).rearrange("p (f c u) -> p f c u", f=TUBE, u=2)
-            for pair in range(2):
+            for half in range(2):
                 bank = banks.tile([P, 2, 2 * P], F32, name="bank")
                 for c in range(2):
                     for u in range(2):
-                        first = ((2 * pair + c) * 2 + u) * P
-                        nc.tensor.transpose(
-                            bank[:, u, c * P : (c + 1) * P], words[:, first : first + P], ident[:]
-                        )
-                nc.scalar.copy(
-                    out=grp[:, ts, pair * 2 * P : (pair + 1) * 2 * P, :],
-                    in_=bank[:].rearrange("p u c -> p c u"),
+                        first = ((2 * half + c) * 2 + u) * P
+                        nc.tensor.transpose(bank[:, u, c * P : (c + 1) * P], words[:, first : first + P], ident[:])
+                nc.scalar.copy(out=target[:, half], in_=bank[:].rearrange("p u c -> p c u"))
+            w_grp[t, ts] = grp
+
+        def quantise_video(t, h, parts=1):
+            cod = work.tile([P, COLUMNS], U32, name="v_cod", align_bytes=64)
+            sca = work.tile([P, COLUMNS], U8, name="v_sca", align_bytes=64)
+            width = COLUMNS // parts
+            for n in range(parts):
+                cols = slice(n * width, (n + 1) * width)
+                nc.vector.quantize_mx(
+                    out=cod[:, cols].bitcast(FP8X4),
+                    scales=sca[:, cols],
+                    in_=v_grp[t, h][:, 4 * n * width : 4 * (n + 1) * width],
                 )
+            v_mx[t, h] = (cod, sca)
 
-        def quantise(t, ts, first=0, last=COLUMNS):
-            if (t, ts) not in codes:
-                cod = work.tile([P, COLUMNS], U32, name="cod%d" % ts, align_bytes=64)
-                sca = work.tile([P, COLUMNS], U8, name="sca%d" % ts, align_bytes=64)
-                codes[t, ts] = cod
-                scales[t, ts] = sca
-            nc.vector.quantize_mx(
-                out=codes[t, ts][:, first:last].bitcast(FP8X4),
-                scales=scales[t, ts][:, first:last],
-                in_=grouped[t][:, (ts * COLUMNS + first) * 4 : (ts * COLUMNS + last) * 4],
-            )
+        def quantise_w(t, ts):
+            cod = work.tile([P, COLUMNS], U32, name="w_cod", align_bytes=64)
+            sca = work.tile([P, COLUMNS], U8, name="w_sca", align_bytes=64)
+            nc.vector.quantize_mx(out=cod[:].bitcast(FP8X4), scales=sca[:], in_=w_grp[t, ts][:])
+            w_mx[t, ts] = (cod, sca)
 
-        def multiply(t, ts, j):
-            tokens = slice(EMBED + j * P, EMBED + (j + 1) * P)
+        def multiply(t, h, pair, ts):
+            v_cod, v_sca = v_mx[t, h]
+            w_cod, w_sca = w_mx[t, ts]
+            first = (pair * TUBE + ts) * P
+            tokens = slice(first, first + P)
             nc.tensor.matmul_mx(
-                out=acc[j][:],
-                lhsT=codes[t, ts][:, tokens].bitcast(FP8X4),
-                lhsT_scale=scales[t, ts][:, tokens],
-                rhs=codes[t, ts][:, 0:EMBED].bitcast(FP8X4),
-                rhs_scale=scales[t, ts][:, 0:EMBED],
+                out=acc[h, pair][:],
+                lhsT=v_cod[:, tokens].bitcast(FP8X4),
+                lhsT_scale=v_sca[:, tokens],
+                rhs=w_cod[:].bitcast(FP8X4),
+                rhs_scale=w_sca[:],
                 start=(t == 0 and ts == 0),
                 stop=(t == BANDS - 1 and ts == TUBE - 1),
             )
 
-        def add_bias(j):
-            part = slice(j * EMBED, (j + 1) * EMBED)
+        def multiply_half(t, h):
+            for ts in range(TUBE):
+                for pair in range(PAIRS):
+                    multiply(t, h, pair, ts)
+
+        def add_bias(pair):
             bank = banks.tile([P, EMBED], F32, name="bank")
-            nc.tensor.matmul(out=bank[:], lhsT=select[:], rhs=pos_sb[:, part], start=True, stop=True)
-            nc.scalar.copy(out=addend[:, part], in_=bank[:])
+            for n in range(2):
+                first = PAIR_TOK * (1 - n)
+                part = slice((2 * pair + n) * EMBED, (2 * pair + n + 1) * EMBED)
+                nc.tensor.matmul(
+                    out=bank[:], lhsT=select[:, first : first + P], rhs=pos_sb[:, part], start=(n == 0), stop=(n == 1)
+                )
+            nc.scalar.copy(out=addend[:, pair * EMBED : (pair + 1) * EMBED], in_=bank[:])
 
-        WEIGHTS, TOKENS = (0, EMBED), (EMBED, COLUMNS)
-
-        def multiply_pass(t, ts):
-            for j in range(GRID):
-                multiply(t, ts, j)
-
+        for pair in range(PAIRS):
+            add_bias(pair)
         regroup_w(0, 0)
-        for h in range(HALVES):
-            regroup(0, h)
+        regroup_video(0, 0)
         regroup_w(0, 1)
-        for t in range(BANDS):
-            grp_t = work.tile([P, TUBE * 4 * COLUMNS], BF16, name="grp", align_bytes=64)
-            grouped[t] = grp_t
-            transpose_w(t, 0)
+        transpose_w(0, 0)
+        transpose_video(0, 0)
+        quantise_w(0, 0)
+        regroup_video(0, 1)
+        transpose_w(0, 1)
+        quantise_video(0, 0)
+        regroup_w(1, 0)
+        transpose_video(0, 1)
+        quantise_w(0, 1)
+        multiply_half(0, 0)
+        transpose_w(1, 0)
+        regroup_video(1, 0)
+        regroup_w(1, 1)
+        quantise_video(0, 1)
+        quantise_w(1, 0)
+        for t in range(1, BANDS):
             transpose_video(t, 0)
-            transpose_video(t, 1)
-            if t >= 1:
-                quantise(t - 1, 0, *TOKENS)
-                quantise(t - 1, 1, *TOKENS)
-                quantise(t - 1, 1, *WEIGHTS)
-                multiply_pass(t - 1, 0)
-            if t + 1 < BANDS:
-                for h in range(HALVES):
-                    regroup(t + 1, h)
-            quantise(t, 0, *WEIGHTS)
-            transpose_video(t, 2)
-            transpose_video(t, 3)
             transpose_w(t, 1)
-            if t >= 1:
-                multiply_pass(t - 1, 1)
+            multiply_half(t - 1, 1)
+            regroup_video(t, 1)
             if t + 1 < BANDS:
-                for ts in range(TUBE):
-                    regroup_w(t + 1, ts)
-            if t == 0:
-                for j in range(GRID):
-                    add_bias(j)
+                regroup_w(t + 1, 0)
+            quantise_video(t, 0)
+            transpose_video(t, 1)
+            if t + 1 < BANDS:
+                transpose_w(t + 1, 0)
+            quantise_w(t, 1)
+            if t + 1 < BANDS:
+                multiply_half(t, 0)
+                regroup_video(t + 1, 0)
+                regroup_w(t + 1, 1)
+            if t + 1 < BANDS:
+                quantise_video(t, 1)
+                quantise_w(t + 1, 0)
 
-        quantise(BANDS - 1, 0, *TOKENS)
-        multiply_pass(BANDS - 1, 0)
-        quantise(BANDS - 1, 1, *TOKENS)
-        quantise(BANDS - 1, 1, *WEIGHTS)
-        for j in range(GRID):
-            multiply(BANDS - 1, 1, j)
-            part = slice(j * EMBED, (j + 1) * EMBED)
+        def finish(h, pair):
+            result = consts.tile([P, EMBED], F32, name="result%d_%d" % (h, pair))
             nc.vector.tensor_tensor(
-                out=addend[:, part], in0=acc[j][:], in1=addend[:, part], op=mybir.AluOpType.add
+                out=result[:],
+                in0=acc[h, pair][:],
+                in1=addend[:, pair * EMBED : (pair + 1) * EMBED],
+                op=mybir.AluOpType.add,
             )
-            nc.sync.dma_start(out=out_rows[:, j, :], in_=addend[:, part])
+            for n, queue in enumerate((nc.sync, nc.scalar)):
+                queue.dma_start(
+                    out=out_rows[h * PAIR_TOK : (h + 1) * PAIR_TOK, 2 * pair + n, :],
+                    in_=result[n * PAIR_TOK : (n + 1) * PAIR_TOK, :],
+                )
+
+        last = BANDS - 1
+        quantise_video(last, 1, PAIRS)
+        for h in range(HALVES):
+            for pair in range(PAIRS):
+                for ts in range(TUBE):
+                    multiply(last, h, pair, ts)
+                finish(h, pair)

@@ -32,7 +32,7 @@ def tile_tubeletembedding_k_kernel(tc, video, W, b, pos_embed, out):
     nc = tc.nc
     video_rows = video.rearrange("b s c (i y) x -> (b s i) (c y x)", i=GRID)
     w_rows = W.rearrange("(c p) k -> p c k", p=P)
-    pos_rows = pos_embed.rearrange("o (q j) e -> (o q) (j e)", j=GRID)
+    pos_rows = pos_embed.rearrange("o (q j n) e -> (o q) n j e", j=PAIRS, n=2)
     out_rows = out.rearrange("b (q j) e -> (b q) j e", j=GRID)
 
     with ExitStack() as ctx:
@@ -43,15 +43,18 @@ def tile_tubeletembedding_k_kernel(tc, video, W, b, pos_embed, out):
         banks = ctx.enter_context(tc.psum_pool(name="banks", bufs=4))
         ctx.enter_context(tc.manual_schedule())
 
-        pos_sb = consts.tile([P, GRID * EMBED], BF16)
+        pos_sb = consts.tile([P, PAIRS * EMBED], BF16)
         nc.vector.memset(pos_sb[:].bitcast(F32), 0.0)
         warm = consts.tile([P, 1], F32)
         nc.vector.memset(warm[:], 0.0)
         nc.scalar.copy(out=warm[:], in_=warm[:])
-        nc.scalar.dma_start(out=pos_sb[0:Q, :], in_=pos_rows)
+        for n in range(2):
+            nc.scalar.dma_start(
+                out=pos_sb[n * Q : (n + 1) * Q, :].rearrange("p (j e) -> p j e", j=PAIRS), in_=pos_rows[:, n]
+            )
         nc.scalar.dma_start(
-            out=pos_sb[Q : Q + 1, :].rearrange("p (j e) -> p j e", j=GRID),
-            in_=b.rearrange("(o j e) -> o j e", o=1, j=1).to_broadcast([1, GRID, EMBED]),
+            out=pos_sb[2 * Q : 2 * Q + 1, :].rearrange("p (j e) -> p j e", j=PAIRS),
+            in_=b.rearrange("(o j e) -> o j e", o=1, j=1).to_broadcast([1, PAIRS, EMBED]),
         )
         v_raw = {}
         w_raw = {}
@@ -81,12 +84,12 @@ def tile_tubeletembedding_k_kernel(tc, video, W, b, pos_embed, out):
             out=perm[:].rearrange("p (f n i) -> p n f i", f=TUBE, i=GRID),
             in_=ident[:].rearrange("p (n f i) -> p n f i", f=TUBE, i=GRID),
         )
-        select = consts.tile([P, 3 * PAIR_TOK], BF16)
-        nc.vector.memset(select[:], 0.0)
-        for batch in range(2):
-            first = PAIR_TOK + batch * Q
-            nc.vector.tensor_copy(out=select[:, first : first + Q], in_=ident[:, 0:Q])
-        nc.vector.memset(select[Q : Q + 1, PAIR_TOK : 2 * PAIR_TOK], 1.0)
+        select = consts.tile([P, P], BF16)
+        for n in range(2):
+            for batch in range(2):
+                first = (2 * n + batch) * Q
+                nc.vector.tensor_copy(out=select[:, first : first + Q], in_=ident[:, n * Q : (n + 1) * Q])
+        nc.vector.memset(select[2 * Q : 2 * Q + 1, :], 1.0)
 
         addend = consts.tile([P, PAIRS * EMBED], F32)
         acc = {}
@@ -133,16 +136,17 @@ def tile_tubeletembedding_k_kernel(tc, video, W, b, pos_embed, out):
                 nc.scalar.copy(out=target[:, pair], in_=bank[:].rearrange("p u f c -> p f c u"))
             v_grp[t, h] = grp
 
-        def transpose_w(t, ts):
+        def transpose_w(t, ts, split=True):
             grp = work.tile([P, 4 * COLUMNS], BF16, name="w_grp", align_bytes=64)
             target = grp[:].bitcast(F32).rearrange("p (n c u) -> p n c u", n=2, u=2)
-            words = w_tok[t, ts][:].bitcast(F32)
+            words = (w_tok[t, ts] if split else w_raw[t, ts])[:].bitcast(F32)
             for half in range(2):
                 bank = banks.tile([P, 2, 2 * P], F32, name="bank")
                 for c in range(2):
                     for u in range(2):
-                        first = ((2 * half + c) * 2 + u) * P
-                        nc.tensor.transpose(bank[:, u, c * P : (c + 1) * P], words[:, first : first + P], ident[:])
+                        run = (2 * half + c) * 2 * P
+                        picked = slice(run + u * P, run + (u + 1) * P) if split else slice(run + u, run + 2 * P, 2)
+                        nc.tensor.transpose(bank[:, u, c * P : (c + 1) * P], words[:, picked], ident[:])
                 nc.scalar.copy(out=target[:, half], in_=bank[:].rearrange("p u c -> p c u"))
             w_grp[t, ts] = grp
 
@@ -186,21 +190,14 @@ def tile_tubeletembedding_k_kernel(tc, video, W, b, pos_embed, out):
                     multiply(t, h, pair, ts)
 
         def add_bias(pair):
+            part = slice(pair * EMBED, (pair + 1) * EMBED)
             bank = banks.tile([P, EMBED], F32, name="bank")
-            for n in range(2):
-                first = PAIR_TOK * (1 - n)
-                part = slice((2 * pair + n) * EMBED, (2 * pair + n + 1) * EMBED)
-                nc.tensor.matmul(
-                    out=bank[:], lhsT=select[:, first : first + P], rhs=pos_sb[:, part], start=(n == 0), stop=(n == 1)
-                )
-            nc.scalar.copy(out=addend[:, pair * EMBED : (pair + 1) * EMBED], in_=bank[:])
+            nc.tensor.matmul(out=bank[:], lhsT=select[:], rhs=pos_sb[:, part], start=True, stop=True)
+            nc.scalar.copy(out=addend[:, part], in_=bank[:])
 
-        for pair in range(PAIRS):
-            add_bias(pair)
-        regroup_w(0, 0)
         regroup_video(0, 0)
         regroup_w(0, 1)
-        transpose_w(0, 0)
+        transpose_w(0, 0, False)
         transpose_video(0, 0)
         quantise_w(0, 0)
         regroup_video(0, 1)
@@ -208,6 +205,8 @@ def tile_tubeletembedding_k_kernel(tc, video, W, b, pos_embed, out):
         quantise_video(0, 0)
         regroup_w(1, 0)
         transpose_video(0, 1)
+        for pair in range(PAIRS):
+            add_bias(pair)
         quantise_w(0, 1)
         multiply_half(0, 0)
         transpose_w(1, 0)

@@ -45,9 +45,9 @@ def tile_tubeletembedding_k_kernel(tc, video, W, b, pos_embed, out):
 
         pos_sb = consts.tile([P, PAIRS * EMBED], BF16)
         nc.vector.memset(pos_sb[:].bitcast(F32), 0.0)
-        warm = consts.tile([P, 1], F32)
-        nc.vector.memset(warm[:], 0.0)
-        nc.scalar.copy(out=warm[:], in_=warm[:])
+        warm = consts.tile([P, 64], F32)
+        nc.vector.memset(warm[:, 0:1], 0.0)
+        nc.scalar.copy(out=warm[:, 0:1], in_=warm[:, 0:1])
         for n in range(2):
             nc.scalar.dma_start(
                 out=pos_sb[n * Q : (n + 1) * Q, :].rearrange("p (j e) -> p j e", j=PAIRS), in_=pos_rows[:, n]
@@ -122,7 +122,7 @@ def tile_tubeletembedding_k_kernel(tc, video, W, b, pos_embed, out):
             w_tok[t, ts] = tok
 
         def transpose_video(t, h):
-            grp = work.tile([P, 4 * COLUMNS], BF16, name="v_grp", align_bytes=64)
+            grp = work.tile([P, 4 * COLUMNS], BF16, name="v_grp", align_bytes=256)
             target = grp[:].bitcast(F32).rearrange("p (j f c u) -> p j f c u", f=TUBE, j=PAIRS, u=2)
             words = v_tok[t, h][:].bitcast(F32)
             for pair in range(PAIRS):
@@ -137,7 +137,7 @@ def tile_tubeletembedding_k_kernel(tc, video, W, b, pos_embed, out):
             v_grp[t, h] = grp
 
         def transpose_w(t, ts, split=True):
-            grp = work.tile([P, 4 * COLUMNS], BF16, name="w_grp", align_bytes=64)
+            grp = work.tile([P, 4 * COLUMNS], BF16, name="w_grp", align_bytes=256)
             target = grp[:].bitcast(F32).rearrange("p (n c u) -> p n c u", n=2, u=2)
             words = (w_tok[t, ts] if split else w_raw[t, ts])[:].bitcast(F32)
             for half in range(2):
@@ -151,8 +151,8 @@ def tile_tubeletembedding_k_kernel(tc, video, W, b, pos_embed, out):
             w_grp[t, ts] = grp
 
         def quantise_video(t, h, parts=1):
-            cod = work.tile([P, COLUMNS], U32, name="v_cod", align_bytes=64)
-            sca = work.tile([P, COLUMNS], U8, name="v_sca", align_bytes=64)
+            cod = work.tile([P, COLUMNS], U32, name="v_cod", align_bytes=256)
+            sca = work.tile([P, COLUMNS], U8, name="v_sca", align_bytes=256)
             width = COLUMNS // parts
             for n in range(parts):
                 cols = slice(n * width, (n + 1) * width)
@@ -164,8 +164,8 @@ def tile_tubeletembedding_k_kernel(tc, video, W, b, pos_embed, out):
             v_mx[t, h] = (cod, sca)
 
         def quantise_w(t, ts):
-            cod = work.tile([P, COLUMNS], U32, name="w_cod", align_bytes=64)
-            sca = work.tile([P, COLUMNS], U8, name="w_sca", align_bytes=64)
+            cod = work.tile([P, COLUMNS], U32, name="w_cod", align_bytes=256)
+            sca = work.tile([P, COLUMNS], U8, name="w_sca", align_bytes=256)
             nc.vector.quantize_mx(out=cod[:].bitcast(FP8X4), scales=sca[:], in_=w_grp[t, ts][:])
             w_mx[t, ts] = (cod, sca)
 

from contextlib import ExitStack

import concourse.mybir as mybir
from concourse.masks import make_identity

BF16 = mybir.dt.bfloat16
F32 = mybir.dt.float32
U32 = mybir.dt.uint32
U8 = mybir.dt.uint8
FP8X4 = mybir.dt.float8_e4m3fn_x4

P = 128
BATCH, STACK, TUBE, IMG, PATCH, EMBED = 4, 16, 2, 256, 64, 512
GRID = IMG // PATCH
TUBES = STACK // TUBE
K = TUBE * PATCH * PATCH
K_FRAME = PATCH * PATCH
K_PASS = 4 * P
BANDS = K_FRAME // K_PASS
BAND_ROWS = PATCH // BANDS
BAND_ROW_PIXELS = BAND_ROWS * IMG
HALVES = 2
PAIRS = 2
PAIR_TOK = P // 2
COLUMNS = 512
Q = TUBES * GRID

FLOPS = 2 * BATCH * TUBES * GRID * GRID * EMBED * K


def tile_tubeletembedding_k_kernel(tc, video, W, b, pos_embed, out):
    nc = tc.nc
    video_rows = video.rearrange("b s c (i y) x -> (b s i) (c y x)", i=GRID)
    w_rows = W.rearrange("(c p) k -> p c k", p=P)
    pos_rows = pos_embed.rearrange("o (q j n) e -> (o q) n j e", j=PAIRS, n=2)
    out_rows = out.rearrange("b (q j) e -> (b q) j e", j=GRID)

    with ExitStack() as ctx:
        consts = ctx.enter_context(tc.tile_pool(name="consts", bufs=1))
        loaded = ctx.enter_context(tc.tile_pool(name="loaded", bufs=1))
        work = ctx.enter_context(tc.tile_pool(name="work", bufs=3))
        sums = ctx.enter_context(tc.psum_pool(name="sums", bufs=1))
        banks = ctx.enter_context(tc.psum_pool(name="banks", bufs=4))
        ctx.enter_context(tc.manual_schedule())

        pos_sb = consts.tile([P, PAIRS * EMBED], BF16)
        nc.vector.memset(pos_sb[:].bitcast(F32), 0.0)
        warm = consts.tile([P, 64], F32)
        nc.vector.memset(warm[:, 0:1], 0.0)
        nc.scalar.copy(out=warm[:, 0:1], in_=warm[:, 0:1])
        for n in range(2):
            nc.scalar.dma_start(
                out=pos_sb[n * Q : (n + 1) * Q, :].rearrange("p (j e) -> p j e", j=PAIRS), in_=pos_rows[:, n]
            )
        nc.scalar.dma_start(
            out=pos_sb[2 * Q : 2 * Q + 1, :].rearrange("p (j e) -> p j e", j=PAIRS),
            in_=b.rearrange("(o j e) -> o j e", o=1, j=1).to_broadcast([1, PAIRS, EMBED]),
        )
        v_raw = {}
        w_raw = {}

        def load_video(t, h):
            v_in = loaded.tile([P, BAND_ROW_PIXELS], BF16, name="v_in%d_%d" % (t, h))
            run = slice(t * BAND_ROW_PIXELS, (t + 1) * BAND_ROW_PIXELS)
            nc.sync.dma_start(out=v_in[:], in_=video_rows[h * P : (h + 1) * P, run])
            v_raw[t, h] = v_in

        def load_w(t, ts):
            first = ts * K_FRAME + t * K_PASS
            w_in = loaded.tile([P, GRID * K_PASS], BF16, name="w_in%d_%d" % (t, ts))
            view = w_in[:].rearrange("p (c k) -> p c k", c=GRID)
            nc.sync.dma_start(out=view, in_=w_rows[:, :, first : first + K_PASS])
            w_raw[t, ts] = w_in

        for t in range(BANDS):
            for n in range(2):
                load_w(t, n)
                load_video(t, n)

        ident = consts.tile([P, P], F32)
        make_identity(nc, ident[:])
        perm = consts.tile([P, P], F32)
        nc.vector.tensor_copy(
            out=perm[:].rearrange("p (f n i) -> p n f i", f=TUBE, i=GRID),
            in_=ident[:].rearrange("p (n f i) -> p n f i", f=TUBE, i=GRID),
        )
        select = consts.tile([P, P], BF16)
        for n in range(2):
            for batch in range(2):
                first = (2 * n + batch) * Q
                nc.vector.tensor_copy(out=select[:, first : first + Q], in_=ident[:, n * Q : (n + 1) * Q])
        nc.vector.memset(select[2 * Q : 2 * Q + 1, :], 1.0)

        addend = consts.tile([P, PAIRS * EMBED], F32)
        acc = {}
        for h in range(HALVES):
            for pair in range(PAIRS):
                acc_q = sums.tile([P, EMBED], F32, name="acc%d_%d" % (h, pair))
                acc[h, pair] = acc_q

        v_tok = {}
        w_tok = {}
        v_grp = {}
        w_grp = {}
        v_mx = {}
        w_mx = {}

        def regroup_video(t, h):
            tok = work.tile([P, BAND_ROW_PIXELS], BF16, name="v_tok")
            nc.vector.tensor_copy(
                out=tok[:].bitcast(F32).rearrange("p (j u y x) -> p j u y x", j=GRID, u=2, y=BAND_ROWS),
                in_=v_raw[t, h][:].bitcast(F32).rearrange("p (y j x u) -> p j u y x", j=GRID, u=2, y=BAND_ROWS),
            )
            v_tok[t, h] = tok

        def regroup_w(t, ts):
            tok = work.tile([P, GRID * K_PASS], BF16, name="w_tok")
            nc.vector.tensor_copy(
                out=tok[:].bitcast(F32).rearrange("p (c u w) -> p c u w", c=GRID, u=2),
                in_=w_raw[t, ts][:].bitcast(F32).rearrange("p (c w u) -> p c u w", c=GRID, u=2),
            )
            w_tok[t, ts] = tok

        def transpose_video(t, h):
            grp = work.tile([P, 4 * COLUMNS], BF16, name="v_grp", align_bytes=256)
            target = grp[:].bitcast(F32).rearrange("p (j f c u) -> p j f c u", f=TUBE, j=PAIRS, u=2)
            words = v_tok[t, h][:].bitcast(F32)
            for pair in range(PAIRS):
                bank = banks.tile([P, 2, TUBE, P], F32, name="bank")
                for n in range(2):
                    for u in range(2):
                        first = ((2 * pair + n) * 2 + u) * P
                        nc.tensor.transpose(
                            bank[:, u, :, n * PAIR_TOK : (n + 1) * PAIR_TOK], words[:, first : first + P], perm[:]
                        )
                nc.scalar.copy(out=target[:, pair], in_=bank[:].rearrange("p u f c -> p f c u"))
            v_grp[t, h] = grp

        def transpose_w(t, ts, split=True):
            grp = work.tile([P, 4 * COLUMNS], BF16, name="w_grp", align_bytes=256)
            target = grp[:].bitcast(F32).rearrange("p (n c u) -> p n c u", n=2, u=2)
            words = (w_tok[t, ts] if split else w_raw[t, ts])[:].bitcast(F32)
            for half in range(2):
                bank = banks.tile([P, 2, 2 * P], F32, name="bank")
                for c in range(2):
                    for u in range(2):
                        run = (2 * half + c) * 2 * P
                        picked = slice(run + u * P, run + (u + 1) * P) if split else slice(run + u, run + 2 * P, 2)
                        nc.tensor.transpose(bank[:, u, c * P : (c + 1) * P], words[:, picked], ident[:])
                nc.scalar.copy(out=target[:, half], in_=bank[:].rearrange("p u c -> p c u"))
            w_grp[t, ts] = grp

        def quantise_video(t, h, parts=1):
            cod = work.tile([P, COLUMNS], U32, name="v_cod", align_bytes=256)
            sca = work.tile([P, COLUMNS], U8, name="v_sca", align_bytes=256)
            width = COLUMNS // parts
            for n in range(parts):
                cols = slice(n * width, (n + 1) * width)
                nc.vector.quantize_mx(
                    out=cod[:, cols].bitcast(FP8X4),
                    scales=sca[:, cols],
                    in_=v_grp[t, h][:, 4 * n * width : 4 * (n + 1) * width],
                )
            v_mx[t, h] = (cod, sca)

        def quantise_w(t, ts):
            cod = work.tile([P, COLUMNS], U32, name="w_cod", align_bytes=256)
            sca = work.tile([P, COLUMNS], U8, name="w_sca", align_bytes=256)
            nc.vector.quantize_mx(out=cod[:].bitcast(FP8X4), scales=sca[:], in_=w_grp[t, ts][:])
            w_mx[t, ts] = (cod, sca)

        def multiply(t, h, pair, ts):
            v_cod, v_sca = v_mx[t, h]
            w_cod, w_sca = w_mx[t, ts]
            first = (pair * TUBE + ts) * P
            tokens = slice(first, first + P)
            nc.tensor.matmul_mx(
                out=acc[h, pair][:],
                lhsT=v_cod[:, tokens].bitcast(FP8X4),
                lhsT_scale=v_sca[:, tokens],
                rhs=w_cod[:].bitcast(FP8X4),
                rhs_scale=w_sca[:],
                start=(t == 0 and ts == 0),
                stop=(t == BANDS - 1 and ts == TUBE - 1),
            )

        def multiply_half(t, h):
            for ts in range(TUBE):
                for pair in range(PAIRS):
                    multiply(t, h, pair, ts)

        def add_bias(pair):
            part = slice(pair * EMBED, (pair + 1) * EMBED)
            bank = banks.tile([P, EMBED], F32, name="bank")
            nc.tensor.matmul(out=bank[:], lhsT=select[:], rhs=pos_sb[:, part], start=True, stop=True)
            nc.scalar.copy(out=addend[:, part], in_=bank[:])

        regroup_video(0, 0)
        regroup_w(0, 1)
        transpose_w(0, 0, False)
        transpose_video(0, 0)
        quantise_w(0, 0)
        regroup_video(0, 1)
        transpose_w(0, 1)
        quantise_video(0, 0)
        regroup_w(1, 0)
        transpose_video(0, 1)
        for pair in range(PAIRS):
            add_bias(pair)
        quantise_w(0, 1)
        multiply_half(0, 0)
        transpose_w(1, 0)
        regroup_video(1, 0)
        regroup_w(1, 1)
        quantise_video(0, 1)
        quantise_w(1, 0)
        for t in range(1, BANDS):
            transpose_video(t, 0)
            transpose_w(t, 1)
            multiply_half(t - 1, 1)
            regroup_video(t, 1)
            if t + 1 < BANDS:
                regroup_w(t + 1, 0)
            quantise_video(t, 0)
            transpose_video(t, 1)
            if t + 1 < BANDS:
                transpose_w(t + 1, 0)
            quantise_w(t, 1)
            if t + 1 < BANDS:
                multiply_half(t, 0)
                regroup_video(t + 1, 0)
                regroup_w(t + 1, 1)
            if t + 1 < BANDS:
                quantise_video(t, 1)
                quantise_w(t + 1, 0)

        def finish(h, pair):
            result = consts.tile([P, EMBED], F32, name="result%d_%d" % (h, pair))
            nc.vector.tensor_tensor(
                out=result[:],
                in0=acc[h, pair][:],
                in1=addend[:, pair * EMBED : (pair + 1) * EMBED],
                op=mybir.AluOpType.add,
            )
            for n, queue in enumerate((nc.sync, nc.scalar)):
                queue.dma_start(
                    out=out_rows[h * PAIR_TOK : (h + 1) * PAIR_TOK, 2 * pair + n, :],
                    in_=result[n * PAIR_TOK : (n + 1) * PAIR_TOK, :],
                )

        last = BANDS - 1
        quantise_video(last, 1, PAIRS)
        for h in range(HALVES):
            for pair in range(PAIRS):
                for ts in range(TUBE):
                    multiply(last, h, pair, ts)
                finish(h, pair)
